import numpy as np
import ml_dtypes


def mxq(x, axis, fmt="e4m3"):
    dtype, down = {"e4m3": (ml_dtypes.float8_e4m3fn, 7), "e5m2": (ml_dtypes.float8_e5m2, 14)}[fmt]
    v = np.moveaxis(np.asarray(x, np.float32).astype(ml_dtypes.bfloat16).astype(np.float64), axis, -1)
    blocks = v.reshape(v.shape[:-1] + (-1, 32))
    amax = np.abs(blocks).max(-1, keepdims=True)
    byte = np.maximum(np.where(amax > 0, np.frexp(amax)[1] - 1 + 127, 0) - down, 1)
    scale = np.exp2(byte - 127.0)
    codes = (blocks / scale).astype(np.float32).astype(dtype).astype(np.float64)
    return np.moveaxis((codes * scale).reshape(v.shape), -1, axis)


WIDE = False


def mx_kscale(k):
    if not WIDE:
        return np.ones(k)
    levels = np.array([10, -10, 5, -5, 0])
    a = np.random.permutation(np.resize(levels, k // 512 * 4)).reshape(k // 512, 4)
    idx = np.arange(k)
    return np.exp2(a[idx // 512, idx % 128 // 32])


BF16 = ml_dtypes.bfloat16


def bf(x):
    return np.asarray(x, np.float32).astype(BF16)


def f64(x):
    return np.asarray(x).astype(np.float64)


B, S, D, E = 4, 1024, 512, 2
K = E * D


def setup_inputs():
    s = mx_kscale(K)
    return {"att": bf(np.random.standard_normal((E, B, S, D)) * 0.3 * s.reshape(E, 1, 1, D)),
            "scene_reps": bf(np.random.standard_normal((B, S, D))),
            "Wo": bf(np.random.standard_normal((D, K)) * 2.0 / np.sqrt(K) / s[None, :]),
            "bo": bf(np.random.standard_normal(D) * 0.1),
            "gamma": bf(1.0 + np.random.standard_normal(D) * 0.1),
            "beta": bf(np.random.standard_normal(D) * 0.1)}


def reference(att, scene_reps, Wo, bo, gamma, beta):
    cat = np.moveaxis(f64(att), 0, 2).reshape(B, S, K)
    fused = (mxq(cat, 2, "e4m3") @ mxq(f64(Wo), 1, "e4m3").T) + f64(bo)
    y = f64(scene_reps) + fused
    mu = y.mean(-1, keepdims=True)
    var = y.var(-1, keepdims=True)
    return (y - mu) / np.sqrt(var + 1e-5) * f64(gamma) + f64(beta)

@@ -1,0 +1,310 @@
+from contextlib import ExitStack
+
+import concourse.mybir as mybir
+from concourse.masks import make_identity
+
+F32 = mybir.dt.float32
+BF16 = mybir.dt.bfloat16
+U32 = mybir.dt.uint32
+U8 = mybir.dt.uint8
+FP8X4 = mybir.dt.float8_e4m3fn_x4
+ALU = mybir.AluOpType
+ACT = mybir.ActivationFunctionType
+
+P = 128
+D = 512
+E = 2
+TOK = 4096
+NT = TOK // P
+G = 4
+NCH = NT // G
+NP = NT // 2
+EPS = 1e-5
+FLOPS = 2 * TOK * E * D * D
+MANUAL = True
+RSQRT = True
+OFFLOAD = tuple(range(NP - 1))
+
+
+def tile_heterogeneousgraphtransformer_pb_t_kernel(tc, att, scene_reps, Wo, bo, gamma, beta, out):
+    nc = tc.nc
+    att_v = att.rearrange("e b s d -> e (b s) d").rearrange("e (p j) d -> p e j d", j=NT)
+    scene_v = scene_reps.rearrange("b s d -> (b s) d").rearrange("(p j) d -> p j d", j=NT)
+    out_v = out.rearrange("b s d -> (b s) d").rearrange("(p j) d -> p j d", j=NT)
+    wo_v = Wo.rearrange("(t p) k -> p t k", p=P)
+
+    with ExitStack() as ctx:
+        const = ctx.enter_context(tc.tile_pool(name="const", bufs=1))
+        loads = ctx.enter_context(tc.tile_pool(name="loads", bufs=NCH))
+        grp_pool = ctx.enter_context(tc.tile_pool(name="grp", bufs=3))
+        code_pool = ctx.enter_context(tc.tile_pool(name="code", bufs=3))
+        sb_pool = ctx.enter_context(tc.tile_pool(name="sb", bufs=5))
+        o_pool = ctx.enter_context(tc.tile_pool(name="o", bufs=10))
+        small = ctx.enter_context(tc.tile_pool(name="small", bufs=4))
+        ps_const = ctx.enter_context(tc.psum_pool(name="psc", bufs=1))
+        ps_xt = ctx.enter_context(tc.psum_pool(name="psx", bufs=2))
+        ps_f = ctx.enter_context(tc.psum_pool(name="psf", bufs=4))
+        if MANUAL:
+            ctx.enter_context(tc.manual_schedule())
+
+        vecs = const.tile([P, 3 * D], BF16)
+        nc.vector.memset(vecs[:], 0.0)
+        ones = const.tile([P, P], BF16)
+        nc.vector.memset(ones[:], 1.0)
+        eps_t = const.tile([P, 1], F32)
+        nc.vector.memset(eps_t[:], EPS)
+        ident = const.tile([P, P], F32)
+        make_identity(nc, ident[:])
+        warm = const.tile([P, 1], F32)
+        nc.scalar.activation(out=warm[:], in_=eps_t[:], func=(ACT.Abs_reciprocal_sqrt if RSQRT else ACT.Sqrt))
+        junk = const.tile([P, D], F32)
+
+        wo_sb = const.tile([P, 4 * E * D], BF16)
+        for h in range(2):
+            nc.sync.dma_start(
+                out=wo_sb[:, h * 2048:(h + 1) * 2048].rearrange("p (t k) -> p t k", t=2),
+                in_=wo_v[:, 2 * h:2 * h + 2, :],
+            )
+        att_t = []
+        scene_t = []
+        for c in range(NCH):
+            a = loads.tile([P, E * G * D], BF16, name="att%d" % c, tag="att")
+            s = loads.tile([P, G * D], BF16, name="scene%d" % c, tag="scene")
+            att_t.append(a)
+            scene_t.append(s)
+            a_v = a[:].rearrange("p (e j d) -> p e j d", e=E, j=G)
+            s_v = s[:].rearrange("p (j d) -> p j d", j=G)
+            if c == 0:
+                nc.sync.dma_start(out=a_v[:, :, 0:2, :], in_=att_v[:, :, 0:2, :])
+                for i, v in enumerate((bo, gamma, beta)):
+                    nc.sync.dma_start(out=vecs[0:1, i * D:(i + 1) * D], in_=v.rearrange("(o d) -> o d", o=1))
+                nc.sync.dma_start(out=s_v, in_=scene_v[:, 0:G, :])
+                nc.sync.dma_start(out=a_v[:, :, 2:4, :], in_=att_v[:, :, 2:4, :])
+            else:
+                nc.sync.dma_start(out=a_v, in_=att_v[:, :, c * G:(c + 1) * G, :])
+                nc.sync.dma_start(out=s_v, in_=scene_v[:, c * G:(c + 1) * G, :])
+
+        wo_f = wo_sb[:].bitcast(F32)
+        wgrp = const.tile([P, E * D * 4], BF16, align_bytes=64)
+        wgrp_f = wgrp[:].bitcast(F32)
+        wcodes = const.tile([P, E * D], U32, align_bytes=64)
+        wscl = const.tile([P, E * D], U8, align_bytes=64)
+        for h in range(2):
+            for e in range(E):
+                wt = ps_f.tile([P, D], F32, name="wt%d%d" % (h, e), tag="f")
+                for dtl in range(2):
+                    for u in range(2):
+                        src = (2 * h + dtl) * 512 + e * 256 + u * 128
+                        nc.tensor.transpose(
+                            out=wt[:, (dtl * 2 + u) * P:(dtl * 2 + u + 1) * P],
+                            in_=wo_f[:, src:src + P],
+                            identity=ident[:],
+                        )
+                dst = wgrp_f[:, e * 1024 + h * 512:e * 1024 + (h + 1) * 512].rearrange(
+                    "p (t r u) -> p t r u", t=2, u=2)
+                srcv = wt[:].rearrange("p (t u r) -> p t r u", t=2, u=2)
+                if e == 0:
+                    nc.vector.tensor_copy(out=dst, in_=srcv)
+                else:
+                    nc.scalar.copy(out=dst, in_=srcv)
+            for e in range(E):
+                w0 = e * D + h * 256
+                nc.vector.quantize_mx(
+                    out=wcodes[:, w0:w0 + 256].bitcast(FP8X4),
+                    scales=wscl[:, w0:w0 + 256],
+                    in_=wgrp[:, 4 * w0:4 * w0 + 1024],
+                )
+
+        xt_t = {}
+        grp_t = {}
+        code_t = {}
+        scl_t = {}
+        sb_t = {}
+        f_t = {}
+        o_t = {}
+        st = {}
+
+        def transposes(k):
+            if k >= NP:
+                return
+            a_f = att_t[k // 2][:].bitcast(F32)
+            for i in range(2):
+                j = 2 * (k % 2) + i
+                xt = ps_xt.tile([P, D], F32, name="xt%d_%d" % (k, i), tag="xt")
+                xt_t[(k, i)] = xt
+                for e in range(E):
+                    for u in range(2):
+                        src = e * (G * 256) + j * 256 + u * 128
+                        nc.tensor.transpose(
+                            out=xt[:, (e * 2 + u) * P:(e * 2 + u + 1) * P],
+                            in_=a_f[:, src:src + P],
+                            identity=ident[:],
+                        )
+
+        def regroup(k, i):
+            if k >= NP:
+                return
+            if i == 0:
+                grp_t[k] = grp_pool.tile([P, 2 * E * P * 4], BF16, name="grp%d" % k, tag="grp", align_bytes=64)
+            g_f = grp_t[k][:].bitcast(F32)
+            nc.scalar.copy(
+                out=g_f[:, i * 512:(i + 1) * 512].rearrange("p (e r u) -> p e r u", e=E, u=2),
+                in_=xt_t[(k, i)][:].rearrange("p (e u r) -> p e r u", e=E, u=2),
+            )
+
+        def quantise(k):
+            if k >= NP:
+                return
+            cd = code_pool.tile([P, 2 * E * P], U32, name="cd%d" % k, tag="cd", align_bytes=64)
+            sc = code_pool.tile([P, 2 * E * P], U8, name="sc%d" % k, tag="sc", align_bytes=64)
+            code_t[k] = cd
+            scl_t[k] = sc
+            nc.vector.quantize_mx(out=cd[:].bitcast(FP8X4), scales=sc[:], in_=grp_t[k][:])
+
+        def matmuls(k):
+            if k >= NP:
+                return
+            for i in range(2):
+                f = ps_f.tile([P, D], F32, name="f%d_%d" % (k, i), tag="f")
+                f_t[(k, i)] = f
+                for e in range(E):
+                    cols = slice(i * E * P + e * P, i * E * P + (e + 1) * P)
+                    nc.tensor.matmul_mx(
+                        out=f[:],
+                        lhsT=code_t[k][:, cols].bitcast(FP8X4),
+                        lhsT_scale=scl_t[k][:, cols],
+                        rhs=wcodes[:, e * D:(e + 1) * D].bitcast(FP8X4),
+                        rhs_scale=wscl[:, e * D:(e + 1) * D],
+                        start=(e == 0),
+                        stop=(e == E - 1),
+                    )
+
+        def add_bias(k, split=False):
+            if k >= NP:
+                return
+            sb = sb_pool.tile([P, 2 * D], F32, name="sb%d" % k, tag="sb")
+            sb_t[k] = sb
+            s0 = 2 * (k % 2) * D
+            sc_ap = scene_t[k // 2]
+            if split:
+                for i in range(2):
+                    nc.gpsimd.tensor_tensor(out=sb[:, i * D:(i + 1) * D], in0=sc_ap[:, s0 + i * D:s0 + (i + 1) * D],
+                                            in1=bo_b[:], op=ALU.add)
+            else:
+                nc.gpsimd.tensor_tensor(
+                    out=sb[:].rearrange("p (j d) -> p j d", j=2),
+                    in0=sc_ap[:, s0:s0 + 2 * D].rearrange("p (j d) -> p j d", j=2),
+                    in1=bo_b[:].unsqueeze(1).to_broadcast([P, 2, D]),
+                    op=ALU.add,
+                )
+
+        def residual(k, i):
+            if i == 0:
+                st[("sums", k)] = small.tile([P, 2], F32, name="sums%d" % k, tag="sums")
+            sb = sb_t[k]
+            nc.vector.scalar_tensor_tensor(
+                out=sb[:, i * D:(i + 1) * D], in0=f_t[(k, i)][:], scalar=1.0,
+                in1=sb[:, i * D:(i + 1) * D], op0=ALU.mult, op1=ALU.add,
+                accum_out=st[("sums", k)][:, i:i + 1],
+            )
+
+        def squares(k, i):
+            if i == 0:
+                st[("negmu", k)] = small.tile([P, 2], F32, name="negmu%d" % k, tag="negmu")
+                st[("ssq", k)] = small.tile([P, 2], F32, name="ssq%d" % k, tag="ssq")
+            negmu = st[("negmu", k)]
+            nc.scalar.activation(out=negmu[:, i:i + 1], in_=st[("sums", k)][:, i:i + 1], func=ACT.Copy, scale=-1.0 / D)
+            nc.scalar.activation(
+                out=junk[:], in_=sb_t[k][:, i * D:(i + 1) * D], func=ACT.Square,
+                bias=negmu[:, i:i + 1], scale=1.0, accum_out=st[("ssq", k)][:, i:i + 1],
+            )
+
+        def inv_std(k):
+            r = small.tile([P, 2], F32, name="rs%d" % k, tag="rs")
+            if RSQRT:
+                nc.scalar.activation(out=r[:], in_=st[("ssq", k)][:], func=ACT.Abs_reciprocal_sqrt,
+                                     bias=eps_t[:], scale=1.0 / D)
+                st[("rstd", k)] = r
+            else:
+                nc.scalar.activation(out=r[:], in_=st[("ssq", k)][:], func=ACT.Sqrt, bias=eps_t[:], scale=1.0 / D)
+                st[("std", k)] = r
+
+        def recip(k):
+            if not RSQRT:
+                rstd = small.tile([P, 2], F32, name="rstd%d" % k, tag="rstd")
+                nc.vector.reciprocal(out=rstd[:], in_=st[("std", k)][:])
+                st[("rstd", k)] = rstd
+
+        def centre_gain(k, i):
+            if i == 0:
+                o_t[k] = o_pool.tile([P, 2 * D], F32, name="o%d" % k, tag="o")
+            nc.vector.scalar_tensor_tensor(
+                out=o_t[k][:, i * D:(i + 1) * D], in0=sb_t[k][:, i * D:(i + 1) * D],
+                scalar=st[("negmu", k)][:, i:i + 1], in1=gamma_ps[:], op0=ALU.add, op1=ALU.mult,
+            )
+
+        def scale_shift_vector(k, i):
+            o = o_t[k][:, i * D:(i + 1) * D]
+            nc.vector.scalar_tensor_tensor(out=o, in0=o, scalar=st[("rstd", k)][:, i:i + 1], in1=beta_ps[:],
+                                           op0=ALU.mult, op1=ALU.add)
+
+        def scale_scalar(k, i):
+            o = o_t[k][:, i * D:(i + 1) * D]
+            nc.scalar.activation(out=o, in_=o, func=ACT.Copy, scale=st[("rstd", k)][:, i:i + 1])
+
+        def shift_gpsimd(k, i):
+            o = o_t[k][:, i * D:(i + 1) * D]
+            nc.gpsimd.tensor_tensor(out=o, in0=o, in1=beta_b[:], op=ALU.add)
+
+        transposes(0)
+        regroup(0, 0)
+        regroup(0, 1)
+        quantise(0)
+        gamma_ps = ps_const.tile([P, D], F32)
+        beta_ps = ps_const.tile([P, D], F32)
+        bo_ps = ps_xt.tile([P, D], F32, name="bo_ps", tag="xt")
+        nc.tensor.matmul(out=bo_ps[:], lhsT=ones[:], rhs=vecs[:, 0:D], start=True, stop=True)
+        nc.tensor.matmul(out=gamma_ps[:], lhsT=ones[:], rhs=vecs[:, D:2 * D], start=True, stop=True)
+        nc.tensor.matmul(out=beta_ps[:], lhsT=ones[:], rhs=vecs[:, 2 * D:3 * D], start=True, stop=True)
+        bo_b = const.tile([P, D], BF16)
+        nc.vector.tensor_copy(out=bo_b[:], in_=bo_ps[:])
+        beta_b = const.tile([P, D], BF16)
+        nc.vector.tensor_copy(out=beta_b[:], in_=beta_ps[:])
+        add_bias(0, split=True)
+        matmuls(0)
+        transposes(1)
+        regroup(1, 0)
+        regroup(1, 1)
+        transposes(2)
+        add_bias(1)
+        add_bias(2)
+
+        for n in range(NP):
+            off = n in OFFLOAD
+            regroup(n + 2, 0)
+            residual(n, 0)
+            squares(n, 0)
+            residual(n, 1)
+            squares(n, 1)
+            inv_std(n)
+            regroup(n + 2, 1)
+            quantise(n + 1)
+            matmuls(n + 1)
+            transposes(n + 3)
+            centre_gain(n, 0)
+            centre_gain(n, 1)
+            recip(n)
+            if off:
+                scale_scalar(n, 0)
+                shift_gpsimd(n, 0)
+                scale_shift_vector(n, 1)
+            else:
+                scale_shift_vector(n, 0)
+                if n == NP - 1:
+                    nc.sync.dma_start(out=out_v[:, 2 * n, :], in_=o_t[n][:, 0:D])
+                scale_shift_vector(n, 1)
+            add_bias(n + 3)
+            if n == NP - 1:
+                nc.sync.dma_start(out=out_v[:, 2 * n + 1, :], in_=o_t[n][:, D:2 * D])
+            else:
+                nc.sync.dma_start(out=out_v[:, 2 * n:2 * n + 2, :], in_=o_t[n][:].rearrange("p (j d) -> p j d", j=2))

@@ -23,7 +23,7 @@ EPS = 1e-5
 FLOPS = 2 * TOK * E * D * D
 MANUAL = True
 RSQRT = True
-OFFLOAD = tuple(range(NP - 1))
+OFFLOAD = ()
 
 
 def tile_heterogeneousgraphtransformer_pb_t_kernel(tc, att, scene_reps, Wo, bo, gamma, beta, out):

@@ -38,7 +38,7 @@ def tile_heterogeneousgraphtransformer_pb_t_kernel(tc, att, scene_reps, Wo, bo, 
         loads = ctx.enter_context(tc.tile_pool(name="loads", bufs=NCH))
         grp_pool = ctx.enter_context(tc.tile_pool(name="grp", bufs=3))
         code_pool = ctx.enter_context(tc.tile_pool(name="code", bufs=3))
-        sb_pool = ctx.enter_context(tc.tile_pool(name="sb", bufs=5))
+        sb_pool = ctx.enter_context(tc.tile_pool(name="sb", bufs=3))
         o_pool = ctx.enter_context(tc.tile_pool(name="o", bufs=10))
         small = ctx.enter_context(tc.tile_pool(name="small", bufs=4))
         ps_const = ctx.enter_context(tc.psum_pool(name="psc", bufs=1))
@@ -179,16 +179,18 @@ def tile_heterogeneousgraphtransformer_pb_t_kernel(tc, att, scene_reps, Wo, bo, 
                         stop=(e == E - 1),
                     )
 
-        def add_bias(k, split=False):
+        def add_bias(k, eng=None):
             if k >= NP:
                 return
+            split = True
+            eng = eng or nc.gpsimd
             sb = sb_pool.tile([P, 2 * D], F32, name="sb%d" % k, tag="sb")
             sb_t[k] = sb
             s0 = 2 * (k % 2) * D
             sc_ap = scene_t[k // 2]
             if split:
                 for i in range(2):
-                    nc.gpsimd.tensor_tensor(out=sb[:, i * D:(i + 1) * D], in0=sc_ap[:, s0 + i * D:s0 + (i + 1) * D],
+                    eng.tensor_tensor(out=sb[:, i * D:(i + 1) * D], in0=sc_ap[:, s0 + i * D:s0 + (i + 1) * D],
                                             in1=bo_b[:], op=ALU.add)
             else:
                 nc.gpsimd.tensor_tensor(
@@ -270,7 +272,7 @@ def tile_heterogeneousgraphtransformer_pb_t_kernel(tc, att, scene_reps, Wo, bo, 
         nc.vector.tensor_copy(out=bo_b[:], in_=bo_ps[:])
         beta_b = const.tile([P, D], BF16)
         nc.vector.tensor_copy(out=beta_b[:], in_=beta_ps[:])
-        add_bias(0, split=True)
+        add_bias(0, nc.vector)
         matmuls(0)
         transposes(1)
         regroup(1, 0)
@@ -288,10 +290,10 @@ def tile_heterogeneousgraphtransformer_pb_t_kernel(tc, att, scene_reps, Wo, bo, 
             squares(n, 1)
             inv_std(n)
             regroup(n + 2, 1)
+            centre_gain(n, 0)
             quantise(n + 1)
             matmuls(n + 1)
             transposes(n + 3)
-            centre_gain(n, 0)
             centre_gain(n, 1)
             recip(n)
             if off:

@@ -38,12 +38,12 @@ def tile_heterogeneousgraphtransformer_pb_t_kernel(tc, att, scene_reps, Wo, bo, 
         loads = ctx.enter_context(tc.tile_pool(name="loads", bufs=NCH))
         grp_pool = ctx.enter_context(tc.tile_pool(name="grp", bufs=3))
         code_pool = ctx.enter_context(tc.tile_pool(name="code", bufs=3))
-        sb_pool = ctx.enter_context(tc.tile_pool(name="sb", bufs=3))
+        sb_pool = ctx.enter_context(tc.tile_pool(name="sb", bufs=4))
         o_pool = ctx.enter_context(tc.tile_pool(name="o", bufs=10))
         small = ctx.enter_context(tc.tile_pool(name="small", bufs=4))
         ps_const = ctx.enter_context(tc.psum_pool(name="psc", bufs=1))
         ps_xt = ctx.enter_context(tc.psum_pool(name="psx", bufs=2))
-        ps_f = ctx.enter_context(tc.psum_pool(name="psf", bufs=4))
+        ps_f = ctx.enter_context(tc.psum_pool(name="psf", bufs=3))
         if MANUAL:
             ctx.enter_context(tc.manual_schedule())
 
@@ -179,19 +179,18 @@ def tile_heterogeneousgraphtransformer_pb_t_kernel(tc, att, scene_reps, Wo, bo, 
                         stop=(e == E - 1),
                     )
 
-        def add_bias(k, eng=None):
+        def add_bias(k, split=True):
             if k >= NP:
                 return
             split = True
-            eng = eng or nc.gpsimd
             sb = sb_pool.tile([P, 2 * D], F32, name="sb%d" % k, tag="sb")
             sb_t[k] = sb
             s0 = 2 * (k % 2) * D
             sc_ap = scene_t[k // 2]
             if split:
                 for i in range(2):
-                    eng.tensor_tensor(out=sb[:, i * D:(i + 1) * D], in0=sc_ap[:, s0 + i * D:s0 + (i + 1) * D],
-                                            in1=bo_b[:], op=ALU.add)
+                    nc.vector.tensor_tensor(out=sb[:, i * D:(i + 1) * D], in0=sc_ap[:, s0 + i * D:s0 + (i + 1) * D],
+                                            in1=bo_ps[:], op=ALU.add)
             else:
                 nc.gpsimd.tensor_tensor(
                     out=sb[:].rearrange("p (j d) -> p j d", j=2),
@@ -264,7 +263,7 @@ def tile_heterogeneousgraphtransformer_pb_t_kernel(tc, att, scene_reps, Wo, bo, 
         quantise(0)
         gamma_ps = ps_const.tile([P, D], F32)
         beta_ps = ps_const.tile([P, D], F32)
-        bo_ps = ps_xt.tile([P, D], F32, name="bo_ps", tag="xt")
+        bo_ps = ps_const.tile([P, D], F32)
         nc.tensor.matmul(out=bo_ps[:], lhsT=ones[:], rhs=vecs[:, 0:D], start=True, stop=True)
         nc.tensor.matmul(out=gamma_ps[:], lhsT=ones[:], rhs=vecs[:, D:2 * D], start=True, stop=True)
         nc.tensor.matmul(out=beta_ps[:], lhsT=ones[:], rhs=vecs[:, 2 * D:3 * D], start=True, stop=True)
@@ -272,14 +271,13 @@ def tile_heterogeneousgraphtransformer_pb_t_kernel(tc, att, scene_reps, Wo, bo, 
         nc.vector.tensor_copy(out=bo_b[:], in_=bo_ps[:])
         beta_b = const.tile([P, D], BF16)
         nc.vector.tensor_copy(out=beta_b[:], in_=beta_ps[:])
-        add_bias(0, nc.vector)
+        add_bias(0, split=True)
         matmuls(0)
         transposes(1)
         regroup(1, 0)
         regroup(1, 1)
         transposes(2)
         add_bias(1)
-        add_bias(2)
 
         for n in range(NP):
             off = n in OFFLOAD
@@ -290,10 +288,10 @@ def tile_heterogeneousgraphtransformer_pb_t_kernel(tc, att, scene_reps, Wo, bo, 
             squares(n, 1)
             inv_std(n)
             regroup(n + 2, 1)
-            centre_gain(n, 0)
             quantise(n + 1)
             matmuls(n + 1)
             transposes(n + 3)
+            centre_gain(n, 0)
             centre_gain(n, 1)
             recip(n)
             if off:
@@ -305,7 +303,7 @@ def tile_heterogeneousgraphtransformer_pb_t_kernel(tc, att, scene_reps, Wo, bo, 
                 if n == NP - 1:
                     nc.sync.dma_start(out=out_v[:, 2 * n, :], in_=o_t[n][:, 0:D])
                 scale_shift_vector(n, 1)
-            add_bias(n + 3)
+            add_bias(n + 2)
             if n == NP - 1:
                 nc.sync.dma_start(out=out_v[:, 2 * n + 1, :], in_=o_t[n][:, D:2 * D])
             else:

@@ -23,7 +23,7 @@ EPS = 1e-5
 FLOPS = 2 * TOK * E * D * D
 MANUAL = True
 RSQRT = True
-OFFLOAD = ()
+OFFLOAD = (0, 2, 4, 6, 8, 10, 12, 14)
 
 
 def tile_heterogeneousgraphtransformer_pb_t_kernel(tc, att, scene_reps, Wo, bo, gamma, beta, out):
@@ -38,12 +38,12 @@ def tile_heterogeneousgraphtransformer_pb_t_kernel(tc, att, scene_reps, Wo, bo, 
         loads = ctx.enter_context(tc.tile_pool(name="loads", bufs=NCH))
         grp_pool = ctx.enter_context(tc.tile_pool(name="grp", bufs=3))
         code_pool = ctx.enter_context(tc.tile_pool(name="code", bufs=3))
-        sb_pool = ctx.enter_context(tc.tile_pool(name="sb", bufs=4))
+        sb_pool = ctx.enter_context(tc.tile_pool(name="sb", bufs=5))
         o_pool = ctx.enter_context(tc.tile_pool(name="o", bufs=10))
         small = ctx.enter_context(tc.tile_pool(name="small", bufs=4))
         ps_const = ctx.enter_context(tc.psum_pool(name="psc", bufs=1))
         ps_xt = ctx.enter_context(tc.psum_pool(name="psx", bufs=2))
-        ps_f = ctx.enter_context(tc.psum_pool(name="psf", bufs=3))
+        ps_f = ctx.enter_context(tc.psum_pool(name="psf", bufs=4))
         if MANUAL:
             ctx.enter_context(tc.manual_schedule())
 
@@ -179,18 +179,17 @@ def tile_heterogeneousgraphtransformer_pb_t_kernel(tc, att, scene_reps, Wo, bo, 
                         stop=(e == E - 1),
                     )
 
-        def add_bias(k, split=True):
+        def add_bias(k, split=False):
             if k >= NP:
                 return
-            split = True
             sb = sb_pool.tile([P, 2 * D], F32, name="sb%d" % k, tag="sb")
             sb_t[k] = sb
             s0 = 2 * (k % 2) * D
             sc_ap = scene_t[k // 2]
             if split:
                 for i in range(2):
-                    nc.vector.tensor_tensor(out=sb[:, i * D:(i + 1) * D], in0=sc_ap[:, s0 + i * D:s0 + (i + 1) * D],
-                                            in1=bo_ps[:], op=ALU.add)
+                    nc.gpsimd.tensor_tensor(out=sb[:, i * D:(i + 1) * D], in0=sc_ap[:, s0 + i * D:s0 + (i + 1) * D],
+                                            in1=bo_b[:], op=ALU.add)
             else:
                 nc.gpsimd.tensor_tensor(
                     out=sb[:].rearrange("p (j d) -> p j d", j=2),
@@ -263,7 +262,7 @@ def tile_heterogeneousgraphtransformer_pb_t_kernel(tc, att, scene_reps, Wo, bo, 
         quantise(0)
         gamma_ps = ps_const.tile([P, D], F32)
         beta_ps = ps_const.tile([P, D], F32)
-        bo_ps = ps_const.tile([P, D], F32)
+        bo_ps = ps_xt.tile([P, D], F32, name="bo_ps", tag="xt")
         nc.tensor.matmul(out=bo_ps[:], lhsT=ones[:], rhs=vecs[:, 0:D], start=True, stop=True)
         nc.tensor.matmul(out=gamma_ps[:], lhsT=ones[:], rhs=vecs[:, D:2 * D], start=True, stop=True)
         nc.tensor.matmul(out=beta_ps[:], lhsT=ones[:], rhs=vecs[:, 2 * D:3 * D], start=True, stop=True)
@@ -278,33 +277,39 @@ def tile_heterogeneousgraphtransformer_pb_t_kernel(tc, att, scene_reps, Wo, bo, 
         regroup(1, 1)
         transposes(2)
         add_bias(1)
+        add_bias(2)
 
-        for n in range(NP):
-            off = n in OFFLOAD
-            regroup(n + 2, 0)
-            residual(n, 0)
-            squares(n, 0)
-            residual(n, 1)
-            squares(n, 1)
-            inv_std(n)
-            regroup(n + 2, 1)
-            quantise(n + 1)
-            matmuls(n + 1)
-            transposes(n + 3)
-            centre_gain(n, 0)
-            centre_gain(n, 1)
-            recip(n)
-            if off:
-                scale_scalar(n, 0)
-                shift_gpsimd(n, 0)
-                scale_shift_vector(n, 1)
-            else:
-                scale_shift_vector(n, 0)
-                if n == NP - 1:
-                    nc.sync.dma_start(out=out_v[:, 2 * n, :], in_=o_t[n][:, 0:D])
-                scale_shift_vector(n, 1)
-            add_bias(n + 2)
-            if n == NP - 1:
-                nc.sync.dma_start(out=out_v[:, 2 * n + 1, :], in_=o_t[n][:, D:2 * D])
-            else:
-                nc.sync.dma_start(out=out_v[:, 2 * n:2 * n + 2, :], in_=o_t[n][:].rearrange("p (j d) -> p j d", j=2))
+        def store(k):
+            nc.sync.dma_start(out=out_v[:, 2 * k:2 * k + 2, :], in_=o_t[k][:].rearrange("p (j d) -> p j d", j=2))
+
+        for n in range(NP + 1):
+            m = n - 1
+            if m >= 0 and m in OFFLOAD:
+                scale_scalar(m, 0)
+                shift_gpsimd(m, 0)
+            if n < NP:
+                regroup(n + 2, 0)
+                residual(n, 0)
+                squares(n, 0)
+                residual(n, 1)
+                squares(n, 1)
+                inv_std(n)
+                regroup(n + 2, 1)
+                quantise(n + 1)
+                matmuls(n + 1)
+                transposes(n + 3)
+            if m >= 0:
+                recip(m)
+                if m not in OFFLOAD:
+                    scale_shift_vector(m, 0)
+                    if m == NP - 1:
+                        nc.sync.dma_start(out=out_v[:, 2 * m, :], in_=o_t[m][:, 0:D])
+                scale_shift_vector(m, 1)
+                if m == NP - 1:
+                    nc.sync.dma_start(out=out_v[:, 2 * m + 1, :], in_=o_t[m][:, D:2 * D])
+                else:
+                    store(m)
+            if n < NP:
+                centre_gain(n, 0)
+                centre_gain(n, 1)
+                add_bias(n + 3)

@@ -203,8 +203,8 @@ def tile_heterogeneousgraphtransformer_pb_t_kernel(tc, att, scene_reps, Wo, bo, 
                 st[("sums", k)] = small.tile([P, 2], F32, name="sums%d" % k, tag="sums")
             sb = sb_t[k]
             nc.vector.scalar_tensor_tensor(
-                out=sb[:, i * D:(i + 1) * D], in0=f_t[(k, i)][:], scalar=1.0,
-                in1=sb[:, i * D:(i + 1) * D], op0=ALU.mult, op1=ALU.add,
+                out=sb[:, i * D:(i + 1) * D], in0=sb[:, i * D:(i + 1) * D], scalar=1.0,
+                in1=f_t[(k, i)][:], op0=ALU.mult, op1=ALU.add,
                 accum_out=st[("sums", k)][:, i:i + 1],
             )
 

@@ -23,7 +23,7 @@ EPS = 1e-5
 FLOPS = 2 * TOK * E * D * D
 MANUAL = True
 RSQRT = True
-OFFLOAD = (0, 2, 4, 6, 8, 10, 12, 14)
+OFFLOAD = ()
 
 
 def tile_heterogeneousgraphtransformer_pb_t_kernel(tc, att, scene_reps, Wo, bo, gamma, beta, out):
@@ -38,7 +38,7 @@ def tile_heterogeneousgraphtransformer_pb_t_kernel(tc, att, scene_reps, Wo, bo, 
         loads = ctx.enter_context(tc.tile_pool(name="loads", bufs=NCH))
         grp_pool = ctx.enter_context(tc.tile_pool(name="grp", bufs=3))
         code_pool = ctx.enter_context(tc.tile_pool(name="code", bufs=3))
-        sb_pool = ctx.enter_context(tc.tile_pool(name="sb", bufs=5))
+        sb_pool = ctx.enter_context(tc.tile_pool(name="sb", bufs=3))
         o_pool = ctx.enter_context(tc.tile_pool(name="o", bufs=10))
         small = ctx.enter_context(tc.tile_pool(name="small", bufs=4))
         ps_const = ctx.enter_context(tc.psum_pool(name="psc", bufs=1))
@@ -179,16 +179,18 @@ def tile_heterogeneousgraphtransformer_pb_t_kernel(tc, att, scene_reps, Wo, bo, 
                         stop=(e == E - 1),
                     )
 
-        def add_bias(k, split=False):
+        def add_bias(k, eng=None):
             if k >= NP:
                 return
+            split = True
+            eng = eng or nc.gpsimd
             sb = sb_pool.tile([P, 2 * D], F32, name="sb%d" % k, tag="sb")
             sb_t[k] = sb
             s0 = 2 * (k % 2) * D
             sc_ap = scene_t[k // 2]
             if split:
                 for i in range(2):
-                    nc.gpsimd.tensor_tensor(out=sb[:, i * D:(i + 1) * D], in0=sc_ap[:, s0 + i * D:s0 + (i + 1) * D],
+                    eng.tensor_tensor(out=sb[:, i * D:(i + 1) * D], in0=sc_ap[:, s0 + i * D:s0 + (i + 1) * D],
                                             in1=bo_b[:], op=ALU.add)
             else:
                 nc.gpsimd.tensor_tensor(
@@ -270,11 +272,13 @@ def tile_heterogeneousgraphtransformer_pb_t_kernel(tc, att, scene_reps, Wo, bo, 
         nc.vector.tensor_copy(out=bo_b[:], in_=bo_ps[:])
         beta_b = const.tile([P, D], BF16)
         nc.vector.tensor_copy(out=beta_b[:], in_=beta_ps[:])
-        add_bias(0, split=True)
+        add_bias(0, nc.vector)
         matmuls(0)
         transposes(1)
         regroup(1, 0)
         regroup(1, 1)
+        quantise(1)
+        matmuls(1)
         transposes(2)
         add_bias(1)
         add_bias(2)
@@ -284,26 +288,22 @@ def tile_heterogeneousgraphtransformer_pb_t_kernel(tc, att, scene_reps, Wo, bo, 
 
         for n in range(NP + 1):
             m = n - 1
-            if m >= 0 and m in OFFLOAD:
-                scale_scalar(m, 0)
-                shift_gpsimd(m, 0)
             if n < NP:
-                regroup(n + 2, 0)
                 residual(n, 0)
                 squares(n, 0)
                 residual(n, 1)
                 squares(n, 1)
                 inv_std(n)
-                regroup(n + 2, 1)
-                quantise(n + 1)
-                matmuls(n + 1)
-                transposes(n + 3)
+                if n == 0:
+                    regroup(2, 0)
+                    regroup(2, 1)
+                    transposes(3)
+                regroup(n + 3, 0)
+                regroup(n + 3, 1)
             if m >= 0:
-                recip(m)
-                if m not in OFFLOAD:
-                    scale_shift_vector(m, 0)
-                    if m == NP - 1:
-                        nc.sync.dma_start(out=out_v[:, 2 * m, :], in_=o_t[m][:, 0:D])
+                scale_shift_vector(m, 0)
+                if m == NP - 1:
+                    nc.sync.dma_start(out=out_v[:, 2 * m, :], in_=o_t[m][:, 0:D])
                 scale_shift_vector(m, 1)
                 if m == NP - 1:
                     nc.sync.dma_start(out=out_v[:, 2 * m + 1, :], in_=o_t[m][:, D:2 * D])
@@ -311,5 +311,8 @@ def tile_heterogeneousgraphtransformer_pb_t_kernel(tc, att, scene_reps, Wo, bo, 
                     store(m)
             if n < NP:
                 centre_gain(n, 0)
+                quantise(n + 2)
+                matmuls(n + 2)
+                transposes(n + 4)
                 centre_gain(n, 1)
                 add_bias(n + 3)

@@ -14,28 +14,26 @@ ACT = mybir.ActivationFunctionType
 P = 128
 D = 512
 E = 2
-TOK = 4096
-NT = TOK // P
-G = 4
-NCH = NT // G
-NP = NT // 2
+TOKENS = 4096
+TILES = TOKENS // P
+PAIRS = TILES // 2
+LOAD_TILES = 4
+LOADS = TILES // LOAD_TILES
+WORDS = D // 2
 EPS = 1e-5
-FLOPS = 2 * TOK * E * D * D
-MANUAL = True
-RSQRT = True
-OFFLOAD = ()
+FLOPS = 2 * TOKENS * E * D * D
 
 
 def tile_heterogeneousgraphtransformer_pb_t_kernel(tc, att, scene_reps, Wo, bo, gamma, beta, out):
     nc = tc.nc
-    att_v = att.rearrange("e b s d -> e (b s) d").rearrange("e (p j) d -> p e j d", j=NT)
-    scene_v = scene_reps.rearrange("b s d -> (b s) d").rearrange("(p j) d -> p j d", j=NT)
-    out_v = out.rearrange("b s d -> (b s) d").rearrange("(p j) d -> p j d", j=NT)
+    att_v = att.rearrange("e b s d -> e (b s) d").rearrange("e (p j) d -> p e j d", j=TILES)
+    scene_v = scene_reps.rearrange("b s d -> (b s) d").rearrange("(p j) d -> p j d", j=TILES)
+    out_v = out.rearrange("b s d -> (b s) d").rearrange("(p j) d -> p j d", j=TILES)
     wo_v = Wo.rearrange("(t p) k -> p t k", p=P)
 
     with ExitStack() as ctx:
         const = ctx.enter_context(tc.tile_pool(name="const", bufs=1))
-        loads = ctx.enter_context(tc.tile_pool(name="loads", bufs=NCH))
+        loads = ctx.enter_context(tc.tile_pool(name="loads", bufs=LOADS))
         grp_pool = ctx.enter_context(tc.tile_pool(name="grp", bufs=3))
         code_pool = ctx.enter_context(tc.tile_pool(name="code", bufs=3))
         sb_pool = ctx.enter_context(tc.tile_pool(name="sb", bufs=3))
@@ -44,8 +42,7 @@ def tile_heterogeneousgraphtransformer_pb_t_kernel(tc, att, scene_reps, Wo, bo, 
         ps_const = ctx.enter_context(tc.psum_pool(name="psc", bufs=1))
         ps_xt = ctx.enter_context(tc.psum_pool(name="psx", bufs=2))
         ps_f = ctx.enter_context(tc.psum_pool(name="psf", bufs=4))
-        if MANUAL:
-            ctx.enter_context(tc.manual_schedule())
+        ctx.enter_context(tc.manual_schedule())
 
         vecs = const.tile([P, 3 * D], BF16)
         nc.vector.memset(vecs[:], 0.0)
@@ -56,33 +53,33 @@ def tile_heterogeneousgraphtransformer_pb_t_kernel(tc, att, scene_reps, Wo, bo, 
         ident = const.tile([P, P], F32)
         make_identity(nc, ident[:])
         warm = const.tile([P, 1], F32)
-        nc.scalar.activation(out=warm[:], in_=eps_t[:], func=(ACT.Abs_reciprocal_sqrt if RSQRT else ACT.Sqrt))
-        junk = const.tile([P, D], F32)
+        nc.scalar.activation(out=warm[:], in_=eps_t[:], func=ACT.Abs_reciprocal_sqrt)
+        squares_out = const.tile([P, D], F32)
 
         wo_sb = const.tile([P, 4 * E * D], BF16)
         for h in range(2):
             nc.sync.dma_start(
-                out=wo_sb[:, h * 2048:(h + 1) * 2048].rearrange("p (t k) -> p t k", t=2),
+                out=wo_sb[:, h * 2 * E * D:(h + 1) * 2 * E * D].rearrange("p (t k) -> p t k", t=2),
                 in_=wo_v[:, 2 * h:2 * h + 2, :],
             )
         att_t = []
         scene_t = []
-        for c in range(NCH):
-            a = loads.tile([P, E * G * D], BF16, name="att%d" % c, tag="att")
-            s = loads.tile([P, G * D], BF16, name="scene%d" % c, tag="scene")
+        for c in range(LOADS):
+            a = loads.tile([P, E * LOAD_TILES * D], BF16, name="att%d" % c, tag="att")
+            s = loads.tile([P, LOAD_TILES * D], BF16, name="scene%d" % c, tag="scene")
             att_t.append(a)
             scene_t.append(s)
-            a_v = a[:].rearrange("p (e j d) -> p e j d", e=E, j=G)
-            s_v = s[:].rearrange("p (j d) -> p j d", j=G)
+            a_v = a[:].rearrange("p (e j d) -> p e j d", e=E, j=LOAD_TILES)
+            s_v = s[:].rearrange("p (j d) -> p j d", j=LOAD_TILES)
             if c == 0:
                 nc.sync.dma_start(out=a_v[:, :, 0:2, :], in_=att_v[:, :, 0:2, :])
                 for i, v in enumerate((bo, gamma, beta)):
                     nc.sync.dma_start(out=vecs[0:1, i * D:(i + 1) * D], in_=v.rearrange("(o d) -> o d", o=1))
-                nc.sync.dma_start(out=s_v, in_=scene_v[:, 0:G, :])
+                nc.sync.dma_start(out=s_v, in_=scene_v[:, 0:LOAD_TILES, :])
                 nc.sync.dma_start(out=a_v[:, :, 2:4, :], in_=att_v[:, :, 2:4, :])
             else:
-                nc.sync.dma_start(out=a_v, in_=att_v[:, :, c * G:(c + 1) * G, :])
-                nc.sync.dma_start(out=s_v, in_=scene_v[:, c * G:(c + 1) * G, :])
+                nc.sync.dma_start(out=a_v, in_=att_v[:, :, c * LOAD_TILES:(c + 1) * LOAD_TILES, :])
+                nc.sync.dma_start(out=s_v, in_=scene_v[:, c * LOAD_TILES:(c + 1) * LOAD_TILES, :])
 
         wo_f = wo_sb[:].bitcast(F32)
         wgrp = const.tile([P, E * D * 4], BF16, align_bytes=64)
@@ -92,27 +89,25 @@ def tile_heterogeneousgraphtransformer_pb_t_kernel(tc, att, scene_reps, Wo, bo, 
         for h in range(2):
             for e in range(E):
                 wt = ps_f.tile([P, D], F32, name="wt%d%d" % (h, e), tag="f")
-                for dtl in range(2):
+                for t in range(2):
                     for u in range(2):
-                        src = (2 * h + dtl) * 512 + e * 256 + u * 128
+                        w0 = (2 * h + t) * E * WORDS + e * WORDS + u * P
                         nc.tensor.transpose(
-                            out=wt[:, (dtl * 2 + u) * P:(dtl * 2 + u + 1) * P],
-                            in_=wo_f[:, src:src + P],
-                            identity=ident[:],
+                            out=wt[:, (t * 2 + u) * P:(t * 2 + u + 1) * P], in_=wo_f[:, w0:w0 + P], identity=ident[:]
                         )
-                dst = wgrp_f[:, e * 1024 + h * 512:e * 1024 + (h + 1) * 512].rearrange(
+                dst = wgrp_f[:, (e * D + h * 2 * P) * 2:(e * D + (h + 1) * 2 * P) * 2].rearrange(
                     "p (t r u) -> p t r u", t=2, u=2)
-                srcv = wt[:].rearrange("p (t u r) -> p t r u", t=2, u=2)
+                src = wt[:].rearrange("p (t u r) -> p t r u", t=2, u=2)
                 if e == 0:
-                    nc.vector.tensor_copy(out=dst, in_=srcv)
+                    nc.vector.tensor_copy(out=dst, in_=src)
                 else:
-                    nc.scalar.copy(out=dst, in_=srcv)
+                    nc.scalar.copy(out=dst, in_=src)
             for e in range(E):
-                w0 = e * D + h * 256
+                c0 = e * D + h * 2 * P
                 nc.vector.quantize_mx(
-                    out=wcodes[:, w0:w0 + 256].bitcast(FP8X4),
-                    scales=wscl[:, w0:w0 + 256],
-                    in_=wgrp[:, 4 * w0:4 * w0 + 1024],
+                    out=wcodes[:, c0:c0 + 2 * P].bitcast(FP8X4),
+                    scales=wscl[:, c0:c0 + 2 * P],
+                    in_=wgrp[:, 4 * c0:4 * (c0 + 2 * P)],
                 )
 
         xt_t = {}
@@ -122,10 +117,13 @@ def tile_heterogeneousgraphtransformer_pb_t_kernel(tc, att, scene_reps, Wo, bo, 
         sb_t = {}
         f_t = {}
         o_t = {}
-        st = {}
+        sums_t = {}
+        negmean_t = {}
+        sumsq_t = {}
+        rstd_t = {}
 
         def transposes(k):
-            if k >= NP:
+            if k >= PAIRS:
                 return
             a_f = att_t[k // 2][:].bitcast(F32)
             for i in range(2):
@@ -134,41 +132,37 @@ def tile_heterogeneousgraphtransformer_pb_t_kernel(tc, att, scene_reps, Wo, bo, 
                 xt_t[(k, i)] = xt
                 for e in range(E):
                     for u in range(2):
-                        src = e * (G * 256) + j * 256 + u * 128
+                        w0 = (e * LOAD_TILES + j) * WORDS + u * P
                         nc.tensor.transpose(
-                            out=xt[:, (e * 2 + u) * P:(e * 2 + u + 1) * P],
-                            in_=a_f[:, src:src + P],
-                            identity=ident[:],
+                            out=xt[:, (e * 2 + u) * P:(e * 2 + u + 1) * P], in_=a_f[:, w0:w0 + P], identity=ident[:]
                         )
 
         def regroup(k, i):
-            if k >= NP:
+            if k >= PAIRS:
                 return
             if i == 0:
                 grp_t[k] = grp_pool.tile([P, 2 * E * P * 4], BF16, name="grp%d" % k, tag="grp", align_bytes=64)
             g_f = grp_t[k][:].bitcast(F32)
             nc.scalar.copy(
-                out=g_f[:, i * 512:(i + 1) * 512].rearrange("p (e r u) -> p e r u", e=E, u=2),
+                out=g_f[:, i * D:(i + 1) * D].rearrange("p (e r u) -> p e r u", e=E, u=2),
                 in_=xt_t[(k, i)][:].rearrange("p (e u r) -> p e r u", e=E, u=2),
             )
 
         def quantise(k):
-            if k >= NP:
+            if k >= PAIRS:
                 return
-            cd = code_pool.tile([P, 2 * E * P], U32, name="cd%d" % k, tag="cd", align_bytes=64)
-            sc = code_pool.tile([P, 2 * E * P], U8, name="sc%d" % k, tag="sc", align_bytes=64)
-            code_t[k] = cd
-            scl_t[k] = sc
-            nc.vector.quantize_mx(out=cd[:].bitcast(FP8X4), scales=sc[:], in_=grp_t[k][:])
+            code_t[k] = code_pool.tile([P, 2 * E * P], U32, name="cd%d" % k, tag="cd", align_bytes=64)
+            scl_t[k] = code_pool.tile([P, 2 * E * P], U8, name="sc%d" % k, tag="sc", align_bytes=64)
+            nc.vector.quantize_mx(out=code_t[k][:].bitcast(FP8X4), scales=scl_t[k][:], in_=grp_t[k][:])
 
         def matmuls(k):
-            if k >= NP:
+            if k >= PAIRS:
                 return
             for i in range(2):
                 f = ps_f.tile([P, D], F32, name="f%d_%d" % (k, i), tag="f")
                 f_t[(k, i)] = f
                 for e in range(E):
-                    cols = slice(i * E * P + e * P, i * E * P + (e + 1) * P)
+                    cols = slice((i * E + e) * P, (i * E + e + 1) * P)
                     nc.tensor.matmul_mx(
                         out=f[:],
                         lhsT=code_t[k][:, cols].bitcast(FP8X4),
@@ -179,84 +173,59 @@ def tile_heterogeneousgraphtransformer_pb_t_kernel(tc, att, scene_reps, Wo, bo, 
                         stop=(e == E - 1),
                     )
 
-        def add_bias(k, eng=None):
-            if k >= NP:
+        def add_bias(k, engine):
+            if k >= PAIRS:
                 return
-            split = True
-            eng = eng or nc.gpsimd
-            sb = sb_pool.tile([P, 2 * D], F32, name="sb%d" % k, tag="sb")
-            sb_t[k] = sb
+            sb_t[k] = sb_pool.tile([P, 2 * D], F32, name="sb%d" % k, tag="sb")
             s0 = 2 * (k % 2) * D
-            sc_ap = scene_t[k // 2]
-            if split:
-                for i in range(2):
-                    eng.tensor_tensor(out=sb[:, i * D:(i + 1) * D], in0=sc_ap[:, s0 + i * D:s0 + (i + 1) * D],
-                                            in1=bo_b[:], op=ALU.add)
-            else:
-                nc.gpsimd.tensor_tensor(
-                    out=sb[:].rearrange("p (j d) -> p j d", j=2),
-                    in0=sc_ap[:, s0:s0 + 2 * D].rearrange("p (j d) -> p j d", j=2),
-                    in1=bo_b[:].unsqueeze(1).to_broadcast([P, 2, D]),
+            for i in range(2):
+                engine.tensor_tensor(
+                    out=sb_t[k][:, i * D:(i + 1) * D],
+                    in0=scene_t[k // 2][:, s0 + i * D:s0 + (i + 1) * D],
+                    in1=bo_b[:],
                     op=ALU.add,
                 )
 
         def residual(k, i):
             if i == 0:
-                st[("sums", k)] = small.tile([P, 2], F32, name="sums%d" % k, tag="sums")
-            sb = sb_t[k]
+                sums_t[k] = small.tile([P, 2], F32, name="sums%d" % k, tag="sums")
+            y = sb_t[k][:, i * D:(i + 1) * D]
             nc.vector.scalar_tensor_tensor(
-                out=sb[:, i * D:(i + 1) * D], in0=sb[:, i * D:(i + 1) * D], scalar=1.0,
-                in1=f_t[(k, i)][:], op0=ALU.mult, op1=ALU.add,
-                accum_out=st[("sums", k)][:, i:i + 1],
+                out=y, in0=y, scalar=1.0, in1=f_t[(k, i)][:], op0=ALU.mult, op1=ALU.add,
+                accum_out=sums_t[k][:, i:i + 1],
             )
 
         def squares(k, i):
             if i == 0:
-                st[("negmu", k)] = small.tile([P, 2], F32, name="negmu%d" % k, tag="negmu")
-                st[("ssq", k)] = small.tile([P, 2], F32, name="ssq%d" % k, tag="ssq")
-            negmu = st[("negmu", k)]
-            nc.scalar.activation(out=negmu[:, i:i + 1], in_=st[("sums", k)][:, i:i + 1], func=ACT.Copy, scale=-1.0 / D)
+                negmean_t[k] = small.tile([P, 2], F32, name="negmean%d" % k, tag="negmean")
+                sumsq_t[k] = small.tile([P, 2], F32, name="sumsq%d" % k, tag="sumsq")
             nc.scalar.activation(
-                out=junk[:], in_=sb_t[k][:, i * D:(i + 1) * D], func=ACT.Square,
-                bias=negmu[:, i:i + 1], scale=1.0, accum_out=st[("ssq", k)][:, i:i + 1],
+                out=negmean_t[k][:, i:i + 1], in_=sums_t[k][:, i:i + 1], func=ACT.Copy, scale=-1.0 / D
+            )
+            nc.scalar.activation(
+                out=squares_out[:], in_=sb_t[k][:, i * D:(i + 1) * D], func=ACT.Square,
+                bias=negmean_t[k][:, i:i + 1], scale=1.0, accum_out=sumsq_t[k][:, i:i + 1],
             )
 
         def inv_std(k):
-            r = small.tile([P, 2], F32, name="rs%d" % k, tag="rs")
-            if RSQRT:
-                nc.scalar.activation(out=r[:], in_=st[("ssq", k)][:], func=ACT.Abs_reciprocal_sqrt,
-                                     bias=eps_t[:], scale=1.0 / D)
-                st[("rstd", k)] = r
-            else:
-                nc.scalar.activation(out=r[:], in_=st[("ssq", k)][:], func=ACT.Sqrt, bias=eps_t[:], scale=1.0 / D)
-                st[("std", k)] = r
-
-        def recip(k):
-            if not RSQRT:
-                rstd = small.tile([P, 2], F32, name="rstd%d" % k, tag="rstd")
-                nc.vector.reciprocal(out=rstd[:], in_=st[("std", k)][:])
-                st[("rstd", k)] = rstd
+            rstd_t[k] = small.tile([P, 2], F32, name="rstd%d" % k, tag="rstd")
+            nc.scalar.activation(
+                out=rstd_t[k][:], in_=sumsq_t[k][:], func=ACT.Abs_reciprocal_sqrt, bias=eps_t[:], scale=1.0 / D
+            )
 
         def centre_gain(k, i):
             if i == 0:
                 o_t[k] = o_pool.tile([P, 2 * D], F32, name="o%d" % k, tag="o")
             nc.vector.scalar_tensor_tensor(
                 out=o_t[k][:, i * D:(i + 1) * D], in0=sb_t[k][:, i * D:(i + 1) * D],
-                scalar=st[("negmu", k)][:, i:i + 1], in1=gamma_ps[:], op0=ALU.add, op1=ALU.mult,
+                scalar=negmean_t[k][:, i:i + 1], in1=gamma_ps[:], op0=ALU.add, op1=ALU.mult,
             )
 
-        def scale_shift_vector(k, i):
+        def scale_shift(k, i):
             o = o_t[k][:, i * D:(i + 1) * D]
-            nc.vector.scalar_tensor_tensor(out=o, in0=o, scalar=st[("rstd", k)][:, i:i + 1], in1=beta_ps[:],
-                                           op0=ALU.mult, op1=ALU.add)
-
-        def scale_scalar(k, i):
-            o = o_t[k][:, i * D:(i + 1) * D]
-            nc.scalar.activation(out=o, in_=o, func=ACT.Copy, scale=st[("rstd", k)][:, i:i + 1])
-
-        def shift_gpsimd(k, i):
-            o = o_t[k][:, i * D:(i + 1) * D]
-            nc.gpsimd.tensor_tensor(out=o, in0=o, in1=beta_b[:], op=ALU.add)
+            nc.vector.scalar_tensor_tensor(
+                out=o, in0=o, scalar=rstd_t[k][:, i:i + 1], in1=beta_ps[:], op0=ALU.mult, op1=ALU.add
+            )
 
         transposes(0)
         regroup(0, 0)
@@ -270,8 +239,6 @@ def tile_heterogeneousgraphtransformer_pb_t_kernel(tc, att, scene_reps, Wo, bo, 
         nc.tensor.matmul(out=beta_ps[:], lhsT=ones[:], rhs=vecs[:, 2 * D:3 * D], start=True, stop=True)
         bo_b = const.tile([P, D], BF16)
         nc.vector.tensor_copy(out=bo_b[:], in_=bo_ps[:])
-        beta_b = const.tile([P, D], BF16)
-        nc.vector.tensor_copy(out=beta_b[:], in_=beta_ps[:])
         add_bias(0, nc.vector)
         matmuls(0)
         transposes(1)
@@ -280,15 +247,12 @@ def tile_heterogeneousgraphtransformer_pb_t_kernel(tc, att, scene_reps, Wo, bo, 
         quantise(1)
         matmuls(1)
         transposes(2)
-        add_bias(1)
-        add_bias(2)
+        add_bias(1, nc.gpsimd)
+        add_bias(2, nc.gpsimd)
 
-        def store(k):
-            nc.sync.dma_start(out=out_v[:, 2 * k:2 * k + 2, :], in_=o_t[k][:].rearrange("p (j d) -> p j d", j=2))
-
-        for n in range(NP + 1):
+        for n in range(PAIRS + 1):
             m = n - 1
-            if n < NP:
+            if n < PAIRS:
                 residual(n, 0)
                 squares(n, 0)
                 residual(n, 1)
@@ -301,18 +265,20 @@ def tile_heterogeneousgraphtransformer_pb_t_kernel(tc, att, scene_reps, Wo, bo, 
                 regroup(n + 3, 0)
                 regroup(n + 3, 1)
             if m >= 0:
-                scale_shift_vector(m, 0)
-                if m == NP - 1:
+                scale_shift(m, 0)
+                if m == PAIRS - 1:
                     nc.sync.dma_start(out=out_v[:, 2 * m, :], in_=o_t[m][:, 0:D])
-                scale_shift_vector(m, 1)
-                if m == NP - 1:
+                scale_shift(m, 1)
+                if m == PAIRS - 1:
                     nc.sync.dma_start(out=out_v[:, 2 * m + 1, :], in_=o_t[m][:, D:2 * D])
                 else:
-                    store(m)
-            if n < NP:
+                    nc.sync.dma_start(
+                        out=out_v[:, 2 * m:2 * m + 2, :], in_=o_t[m][:].rearrange("p (j d) -> p j d", j=2)
+                    )
+            if n < PAIRS:
                 centre_gain(n, 0)
                 quantise(n + 2)
                 matmuls(n + 2)
                 transposes(n + 4)
                 centre_gain(n, 1)
-                add_bias(n + 3)
+                add_bias(n + 3, nc.gpsimd)

from contextlib import ExitStack

import concourse.mybir as mybir
from concourse.masks import make_identity

F32 = mybir.dt.float32
BF16 = mybir.dt.bfloat16
U32 = mybir.dt.uint32
U8 = mybir.dt.uint8
FP8X4 = mybir.dt.float8_e4m3fn_x4
ALU = mybir.AluOpType
ACT = mybir.ActivationFunctionType

P = 128
D = 512
E = 2
TOKENS = 4096
TILES = TOKENS // P
PAIRS = TILES // 2
LOAD_TILES = 4
LOADS = TILES // LOAD_TILES
WORDS = D // 2
EPS = 1e-5
FLOPS = 2 * TOKENS * E * D * D


def tile_heterogeneousgraphtransformer_pb_t_kernel(tc, att, scene_reps, Wo, bo, gamma, beta, out):
    nc = tc.nc
    att_v = att.rearrange("e b s d -> e (b s) d").rearrange("e (p j) d -> p e j d", j=TILES)
    scene_v = scene_reps.rearrange("b s d -> (b s) d").rearrange("(p j) d -> p j d", j=TILES)
    out_v = out.rearrange("b s d -> (b s) d").rearrange("(p j) d -> p j d", j=TILES)
    wo_v = Wo.rearrange("(t p) k -> p t k", p=P)

    with ExitStack() as ctx:
        const = ctx.enter_context(tc.tile_pool(name="const", bufs=1))
        loads = ctx.enter_context(tc.tile_pool(name="loads", bufs=LOADS))
        grp_pool = ctx.enter_context(tc.tile_pool(name="grp", bufs=3))
        code_pool = ctx.enter_context(tc.tile_pool(name="code", bufs=3))
        sb_pool = ctx.enter_context(tc.tile_pool(name="sb", bufs=3))
        o_pool = ctx.enter_context(tc.tile_pool(name="o", bufs=10))
        small = ctx.enter_context(tc.tile_pool(name="small", bufs=4))
        ps_const = ctx.enter_context(tc.psum_pool(name="psc", bufs=1))
        ps_xt = ctx.enter_context(tc.psum_pool(name="psx", bufs=2))
        ps_f = ctx.enter_context(tc.psum_pool(name="psf", bufs=4))
        ctx.enter_context(tc.manual_schedule())

        vecs = const.tile([P, 3 * D], BF16)
        nc.vector.memset(vecs[:], 0.0)
        ones = const.tile([P, P], BF16)
        nc.vector.memset(ones[:], 1.0)
        eps_t = const.tile([P, 1], F32)
        nc.vector.memset(eps_t[:], EPS)
        ident = const.tile([P, P], F32)
        make_identity(nc, ident[:])
        warm = const.tile([P, 1], F32)
        nc.scalar.activation(out=warm[:], in_=eps_t[:], func=ACT.Abs_reciprocal_sqrt)
        squares_out = const.tile([P, D], F32)

        wo_sb = const.tile([P, 4 * E * D], BF16)
        for h in range(2):
            nc.sync.dma_start(
                out=wo_sb[:, h * 2 * E * D:(h + 1) * 2 * E * D].rearrange("p (t k) -> p t k", t=2),
                in_=wo_v[:, 2 * h:2 * h + 2, :],
            )
        att_t = []
        scene_t = []
        for c in range(LOADS):
            a = loads.tile([P, E * LOAD_TILES * D], BF16, name="att%d" % c, tag="att")
            s = loads.tile([P, LOAD_TILES * D], BF16, name="scene%d" % c, tag="scene")
            att_t.append(a)
            scene_t.append(s)
            a_v = a[:].rearrange("p (e j d) -> p e j d", e=E, j=LOAD_TILES)
            s_v = s[:].rearrange("p (j d) -> p j d", j=LOAD_TILES)
            if c == 0:
                nc.sync.dma_start(out=a_v[:, :, 0:2, :], in_=att_v[:, :, 0:2, :])
                for i, v in enumerate((bo, gamma, beta)):
                    nc.sync.dma_start(out=vecs[0:1, i * D:(i + 1) * D], in_=v.rearrange("(o d) -> o d", o=1))
                nc.sync.dma_start(out=s_v, in_=scene_v[:, 0:LOAD_TILES, :])
                nc.sync.dma_start(out=a_v[:, :, 2:4, :], in_=att_v[:, :, 2:4, :])
            else:
                nc.sync.dma_start(out=a_v, in_=att_v[:, :, c * LOAD_TILES:(c + 1) * LOAD_TILES, :])
                nc.sync.dma_start(out=s_v, in_=scene_v[:, c * LOAD_TILES:(c + 1) * LOAD_TILES, :])

        wo_f = wo_sb[:].bitcast(F32)
        wgrp = const.tile([P, E * D * 4], BF16, align_bytes=64)
        wgrp_f = wgrp[:].bitcast(F32)
        wcodes = const.tile([P, E * D], U32, align_bytes=64)
        wscl = const.tile([P, E * D], U8, align_bytes=64)
        for h in range(2):
            for e in range(E):
                wt = ps_f.tile([P, D], F32, name="wt%d%d" % (h, e), tag="f")
                for t in range(2):
                    for u in range(2):
                        w0 = (2 * h + t) * E * WORDS + e * WORDS + u * P
                        nc.tensor.transpose(
                            out=wt[:, (t * 2 + u) * P:(t * 2 + u + 1) * P], in_=wo_f[:, w0:w0 + P], identity=ident[:]
                        )
                dst = wgrp_f[:, (e * D + h * 2 * P) * 2:(e * D + (h + 1) * 2 * P) * 2].rearrange(
                    "p (t r u) -> p t r u", t=2, u=2)
                src = wt[:].rearrange("p (t u r) -> p t r u", t=2, u=2)
                if e == 0:
                    nc.vector.tensor_copy(out=dst, in_=src)
                else:
                    nc.scalar.copy(out=dst, in_=src)
            for e in range(E):
                c0 = e * D + h * 2 * P
                nc.vector.quantize_mx(
                    out=wcodes[:, c0:c0 + 2 * P].bitcast(FP8X4),
                    scales=wscl[:, c0:c0 + 2 * P],
                    in_=wgrp[:, 4 * c0:4 * (c0 + 2 * P)],
                )

        xt_t = {}
        grp_t = {}
        code_t = {}
        scl_t = {}
        sb_t = {}
        f_t = {}
        o_t = {}
        sums_t = {}
        negmean_t = {}
        sumsq_t = {}
        rstd_t = {}

        def transposes(k):
            if k >= PAIRS:
                return
            a_f = att_t[k // 2][:].bitcast(F32)
            for i in range(2):
                j = 2 * (k % 2) + i
                xt = ps_xt.tile([P, D], F32, name="xt%d_%d" % (k, i), tag="xt")
                xt_t[(k, i)] = xt
                for e in range(E):
                    for u in range(2):
                        w0 = (e * LOAD_TILES + j) * WORDS + u * P
                        nc.tensor.transpose(
                            out=xt[:, (e * 2 + u) * P:(e * 2 + u + 1) * P], in_=a_f[:, w0:w0 + P], identity=ident[:]
                        )

        def regroup(k, i):
            if k >= PAIRS:
                return
            if i == 0:
                grp_t[k] = grp_pool.tile([P, 2 * E * P * 4], BF16, name="grp%d" % k, tag="grp", align_bytes=64)
            g_f = grp_t[k][:].bitcast(F32)
            nc.scalar.copy(
                out=g_f[:, i * D:(i + 1) * D].rearrange("p (e r u) -> p e r u", e=E, u=2),
                in_=xt_t[(k, i)][:].rearrange("p (e u r) -> p e r u", e=E, u=2),
            )

        def quantise(k):
            if k >= PAIRS:
                return
            code_t[k] = code_pool.tile([P, 2 * E * P], U32, name="cd%d" % k, tag="cd", align_bytes=64)
            scl_t[k] = code_pool.tile([P, 2 * E * P], U8, name="sc%d" % k, tag="sc", align_bytes=64)
            nc.vector.quantize_mx(out=code_t[k][:].bitcast(FP8X4), scales=scl_t[k][:], in_=grp_t[k][:])

        def matmuls(k):
            if k >= PAIRS:
                return
            for i in range(2):
                f = ps_f.tile([P, D], F32, name="f%d_%d" % (k, i), tag="f")
                f_t[(k, i)] = f
                for e in range(E):
                    cols = slice((i * E + e) * P, (i * E + e + 1) * P)
                    nc.tensor.matmul_mx(
                        out=f[:],
                        lhsT=code_t[k][:, cols].bitcast(FP8X4),
                        lhsT_scale=scl_t[k][:, cols],
                        rhs=wcodes[:, e * D:(e + 1) * D].bitcast(FP8X4),
                        rhs_scale=wscl[:, e * D:(e + 1) * D],
                        start=(e == 0),
                        stop=(e == E - 1),
                    )

        def add_bias(k, engine):
            if k >= PAIRS:
                return
            sb_t[k] = sb_pool.tile([P, 2 * D], F32, name="sb%d" % k, tag="sb")
            s0 = 2 * (k % 2) * D
            for i in range(2):
                engine.tensor_tensor(
                    out=sb_t[k][:, i * D:(i + 1) * D],
                    in0=scene_t[k // 2][:, s0 + i * D:s0 + (i + 1) * D],
                    in1=bo_b[:],
                    op=ALU.add,
                )

        def residual(k, i):
            if i == 0:
                sums_t[k] = small.tile([P, 2], F32, name="sums%d" % k, tag="sums")
            y = sb_t[k][:, i * D:(i + 1) * D]
            nc.vector.scalar_tensor_tensor(
                out=y, in0=y, scalar=1.0, in1=f_t[(k, i)][:], op0=ALU.mult, op1=ALU.add,
                accum_out=sums_t[k][:, i:i + 1],
            )

        def squares(k, i):
            if i == 0:
                negmean_t[k] = small.tile([P, 2], F32, name="negmean%d" % k, tag="negmean")
                sumsq_t[k] = small.tile([P, 2], F32, name="sumsq%d" % k, tag="sumsq")
            nc.scalar.activation(
                out=negmean_t[k][:, i:i + 1], in_=sums_t[k][:, i:i + 1], func=ACT.Copy, scale=-1.0 / D
            )
            nc.scalar.activation(
                out=squares_out[:], in_=sb_t[k][:, i * D:(i + 1) * D], func=ACT.Square,
                bias=negmean_t[k][:, i:i + 1], scale=1.0, accum_out=sumsq_t[k][:, i:i + 1],
            )

        def inv_std(k):
            rstd_t[k] = small.tile([P, 2], F32, name="rstd%d" % k, tag="rstd")
            nc.scalar.activation(
                out=rstd_t[k][:], in_=sumsq_t[k][:], func=ACT.Abs_reciprocal_sqrt, bias=eps_t[:], scale=1.0 / D
            )

        def centre_gain(k, i):
            if i == 0:
                o_t[k] = o_pool.tile([P, 2 * D], F32, name="o%d" % k, tag="o")
            nc.vector.scalar_tensor_tensor(
                out=o_t[k][:, i * D:(i + 1) * D], in0=sb_t[k][:, i * D:(i + 1) * D],
                scalar=negmean_t[k][:, i:i + 1], in1=gamma_ps[:], op0=ALU.add, op1=ALU.mult,
            )

        def scale_shift(k, i):
            o = o_t[k][:, i * D:(i + 1) * D]
            nc.vector.scalar_tensor_tensor(
                out=o, in0=o, scalar=rstd_t[k][:, i:i + 1], in1=beta_ps[:], op0=ALU.mult, op1=ALU.add
            )

        transposes(0)
        regroup(0, 0)
        regroup(0, 1)
        quantise(0)
        gamma_ps = ps_const.tile([P, D], F32)
        beta_ps = ps_const.tile([P, D], F32)
        bo_ps = ps_xt.tile([P, D], F32, name="bo_ps", tag="xt")
        nc.tensor.matmul(out=bo_ps[:], lhsT=ones[:], rhs=vecs[:, 0:D], start=True, stop=True)
        nc.tensor.matmul(out=gamma_ps[:], lhsT=ones[:], rhs=vecs[:, D:2 * D], start=True, stop=True)
        nc.tensor.matmul(out=beta_ps[:], lhsT=ones[:], rhs=vecs[:, 2 * D:3 * D], start=True, stop=True)
        bo_b = const.tile([P, D], BF16)
        nc.vector.tensor_copy(out=bo_b[:], in_=bo_ps[:])
        add_bias(0, nc.vector)
        matmuls(0)
        transposes(1)
        regroup(1, 0)
        regroup(1, 1)
        quantise(1)
        matmuls(1)
        transposes(2)
        add_bias(1, nc.gpsimd)
        add_bias(2, nc.gpsimd)

        for n in range(PAIRS + 1):
            m = n - 1
            if n < PAIRS:
                residual(n, 0)
                squares(n, 0)
                residual(n, 1)
                squares(n, 1)
                inv_std(n)
                if n == 0:
                    regroup(2, 0)
                    regroup(2, 1)
                    transposes(3)
                regroup(n + 3, 0)
                regroup(n + 3, 1)
            if m >= 0:
                scale_shift(m, 0)
                if m == PAIRS - 1:
                    nc.sync.dma_start(out=out_v[:, 2 * m, :], in_=o_t[m][:, 0:D])
                scale_shift(m, 1)
                if m == PAIRS - 1:
                    nc.sync.dma_start(out=out_v[:, 2 * m + 1, :], in_=o_t[m][:, D:2 * D])
                else:
                    nc.sync.dma_start(
                        out=out_v[:, 2 * m:2 * m + 2, :], in_=o_t[m][:].rearrange("p (j d) -> p j d", j=2)
                    )
            if n < PAIRS:
                centre_gain(n, 0)
                quantise(n + 2)
                matmuls(n + 2)
                transposes(n + 4)
                centre_gain(n, 1)
                add_bias(n + 3, nc.gpsimd)
